import numpy as np
import ml_dtypes


def mxq(x, axis, fmt="e4m3"):
    dtype, down = {"e4m3": (ml_dtypes.float8_e4m3fn, 7), "e5m2": (ml_dtypes.float8_e5m2, 14)}[fmt]
    v = np.moveaxis(np.asarray(x, np.float32).astype(ml_dtypes.bfloat16).astype(np.float64), axis, -1)
    blocks = v.reshape(v.shape[:-1] + (-1, 32))
    amax = np.abs(blocks).max(-1, keepdims=True)
    byte = np.maximum(np.where(amax > 0, np.frexp(amax)[1] - 1 + 127, 0) - down, 1)
    scale = np.exp2(byte - 127.0)
    codes = (blocks / scale).astype(np.float32).astype(dtype).astype(np.float64)
    return np.moveaxis((codes * scale).reshape(v.shape), -1, axis)


WIDE = False


def mx_kscale(k):
    if not WIDE:
        return np.ones(k)
    levels = np.array([10, -10, 5, -5, 0])
    if k % 512:
        return np.exp2(np.random.permutation(np.resize(levels, k // 32))).repeat(32)
    a = np.empty((k // 512, 16))
    for p in range(k // 512):
        a[p, :8] = np.random.permutation(np.resize(levels, 8))
        for g in range(8):
            far = levels[np.abs(levels - a[p, g]) >= 10]
            a[p, g + 8] = far[np.random.randint(len(far))]
    return np.exp2(a.ravel()).repeat(32)


BF16 = ml_dtypes.bfloat16


def bf(x):
    return np.asarray(x, np.float32).astype(BF16)


def f64(x):
    return np.asarray(x).astype(np.float64)


B, H, G, S, D = 8, 8, 2, 512, 128
R = H // G
LAYER_NUMBER = 1
NORM_FACTOR = np.sqrt(D) * LAYER_NUMBER
COEFF = float(LAYER_NUMBER)


def setup_inputs():
    s = mx_kscale(S)
    return {"query_layer": bf(np.random.standard_normal((B, H, S, D)) * 1.5),
            "key_layer": bf(np.random.standard_normal((B, G, S, D))),
            "value_layer": bf(np.random.standard_normal((B, G, S, D)) * (s.max() / s)[:, None]),
            "attention_mask": bf(np.random.standard_normal((B, 1, S, S)) * 0.5 + np.log(s))}


def reference(query_layer, key_layer, value_layer, attention_mask):
    q = f64(query_layer).reshape(B, G, R, S, D)
    k = f64(key_layer)
    scores = q @ k[:, :, None].transpose(0, 1, 2, 4, 3) / NORM_FACTOR
    scores = scores * COEFF
    scores = scores + f64(attention_mask)[:, :, None, :, :]
    e = np.exp(scores - scores.max(-1, keepdims=True))
    out = (mxq(e, 4, "e4m3") @ mxq(f64(value_layer), 2, "e4m3")[:, :, None]) / e.sum(-1, keepdims=True)
    return out.reshape(B, H, S, D)

@@ -1,0 +1,363 @@
+import math
+from contextlib import ExitStack
+
+import concourse.mybir as mybir
+from concourse.masks import make_identity
+
+BF16 = mybir.dt.bfloat16
+F32 = mybir.dt.float32
+U32 = mybir.dt.uint32
+U8 = mybir.dt.uint8
+FP8X4 = mybir.dt.float8_e4m3fn_x4
+ALU = mybir.AluOpType
+ACT = mybir.ActivationFunctionType
+AX = mybir.AxisListType
+
+B, H, G, S, D = 8, 8, 2, 512, 128
+P = 128
+NT = S // P
+NH = B * H
+NM = 3
+FLOPS = 2 * 2 * B * H * S * S * D
+
+
+def tile_selfattention_t_kernel(tc, query_layer, key_layer, value_layer, attention_mask, out):
+    nc = tc.nc
+    c = 1.0 / math.sqrt(D)
+    with ExitStack() as ctx:
+        ctx.enter_context(tc.manual_schedule())
+        const = ctx.enter_context(tc.tile_pool(name="const", bufs=1))
+        loads = ctx.enter_context(tc.tile_pool(name="loads", bufs=2))
+        batch = ctx.enter_context(tc.tile_pool(name="batch", bufs=2))
+        work = ctx.enter_context(tc.tile_pool(name="work", bufs=2))
+        ps_s = ctx.enter_context(tc.psum_pool(name="ps_s", bufs=4))
+        ps_e = ctx.enter_context(tc.psum_pool(name="ps_e", bufs=2))
+        ps_o = ctx.enter_context(tc.psum_pool(name="ps_o", bufs=1))
+        ps_p = ctx.enter_context(tc.psum_pool(name="ps_p", bufs=1))
+
+        ident_b = const.tile([P, P], BF16, name="ident_b")
+        make_identity(nc, ident_b[:])
+        ident_f = const.tile([P, P], F32, name="ident_f")
+        make_identity(nc, ident_f[:])
+
+        k_sb, m_sb, q_sb, v_sb = {}, {}, {}, {}
+        kT, mt, vc, vs = {}, {}, {}, {}
+        qT, sp, s_sb, e_sb, ep, grp, codes, scales = {}, {}, {}, {}, {}, {}, {}, {}
+        mx, nb, nbv, rs, ri, o_ps = {}, {}, {}, {}, {}, {}
+        prep = {}
+
+        def live(n):
+            return 0 <= n < NH
+
+        def load_k(b):
+            if b >= B:
+                return
+            k_sb[b] = loads.tile([P, G * NT, D], BF16, name="k_sb", tag="k_sb")
+            nc.sync.dma_start(out=k_sb[b][:].rearrange("p (g t) d -> p g (t d)", t=NT), in_=key_layer[b].rearrange("g (p t) d -> p g (t d)", t=NT))
+
+        def load_m(b):
+            if b >= B:
+                return
+            m_sb[b] = loads.tile([P, NT, S], BF16, name="m_sb", tag="m_sb", bufs=3)
+            nc.sync.dma_start(out=m_sb[b][:], in_=attention_mask[b, 0].rearrange("(p j) k -> p j k", j=NT))
+
+        def load_q(b):
+            if b >= B:
+                return
+            q_sb[b] = loads.tile([P, H, NT * D], BF16, name="q_sb", tag="q_sb")
+            nc.sync.dma_start(out=q_sb[b][:], in_=query_layer[b].rearrange("h (p j) d -> p h (j d)", j=NT))
+
+        def load_q_part(h0, h1):
+            if h0 == 0:
+                q_sb[0] = loads.tile([P, H, NT * D], BF16, name="q_sb", tag="q_sb")
+            nc.sync.dma_start(
+                out=q_sb[0][:, h0:h1, :], in_=query_layer[0, h0:h1].rearrange("h (p j) d -> p h (j d)", j=NT)
+            )
+
+        def load_v(b):
+            if b >= B:
+                return
+            v_sb[b] = loads.tile([P, G * NT, D], BF16, name="v_sb", tag="v_sb")
+            nc.sync.dma_start(
+                out=v_sb[b][:].rearrange("p (g t) d -> p g (t d)", t=NT),
+                in_=value_layer[b].rearrange("g (p t) d -> p g (t d)", t=NT),
+            )
+
+        def prep_pe(b, i, pool=None, tag="prep"):
+            pt = (ps_p if pool is None else pool).tile([P, 2, NT, P], BF16, name="prep", tag=tag)
+            prep[(b, i)] = pt
+            if i == 0:
+                for a in range(2):
+                    for j in range(NT):
+                        nc.tensor.transpose(out=pt[:, a, j, :], in_=k_sb[b][:, a * NT + j, :], identity=ident_b[:])
+            else:
+                words = pt[:].rearrange("p a j i -> p (a j i)").bitcast(F32)
+                for j in range(NM):
+                    nc.tensor.transpose(
+                        out=words[:, j * P : (j + 1) * P],
+                        in_=m_sb[b][:, j, :].bitcast(F32)[:, i - 1 : S // 2 : 2],
+                        identity=ident_f[:],
+                    )
+
+        def prep_ev(b, i, part, eng):
+            pt = prep[(b, i)]
+            if i == 0:
+                if part == 0:
+                    kT[b] = batch.tile([P, G, S], BF16, name="kT", tag="kT")
+                    dst = kT[b][:].rearrange("p g s -> p (g s)")
+                    src = pt[:].rearrange("p a j i -> p (a j i)")
+                    nc.scalar.copy(out=dst, in_=src)
+                return
+            if i == 1 and part == 0:
+                mt[b] = batch.tile([P, NT, NM, P], F32, name="mt", tag="mt")
+            kb = 2 * (i - 1) + part
+            dst = mt[b][:, kb, :, :].rearrange("p j i -> p (j i)")
+            src = pt[:].rearrange("p a j i -> p (a j i)")[:, 0 : 2 * NM * P].rearrange("p (n e) -> p n e", e=2)[:, :, part]
+            if eng == "S":
+                nc.scalar.mul(out=dst, in_=src, mul=math.sqrt(D))
+            else:
+                nc.vector.tensor_scalar_mul(out=dst, in0=src, scalar1=math.sqrt(D))
+
+        def prep_v(b):
+            vg = batch.tile([P, G, D, 4], BF16, name="vg", tag="vg", align_bytes=64)
+            nc.vector.tensor_copy(out=vg[:], in_=v_sb[b][:].rearrange("p (g t) d -> p g d t", g=G))
+            vc[b] = batch.tile([P, G * D], U32, name="vc", tag="vc", align_bytes=64)
+            vs[b] = batch.tile([P, G * D], U8, name="vs", tag="vs", align_bytes=64)
+            nc.vector.quantize_mx(
+                out=vc[b][:].bitcast(FP8X4), scales=vs[b][:], in_=vg[:].rearrange("p g d t -> p (g d t)")
+            )
+
+        def qt_pe(n, pool=None, tag="prep"):
+            pt = (ps_p if pool is None else pool).tile([P, 2, NT, P], BF16, name="prep", tag=tag)
+            prep[("q", n)] = pt
+            for a in range(2):
+                for j in range(NT):
+                    nc.tensor.transpose(
+                        out=pt[:, a, j, :],
+                        in_=q_sb[(n + a) // H][:, (n + a) % H, j * D : (j + 1) * D],
+                        identity=ident_b[:],
+                    )
+
+        def qt_ev(n, eng):
+            qT[n // 2] = work.tile([P, 2, NT, P], BF16, name="qT", tag="qT", bufs=3)
+            dst = qT[n // 2][:].rearrange("p a j i -> p (a j i)")
+            src = prep[("q", n)][:].rearrange("p a j i -> p (a j i)")
+            if eng == "S":
+                nc.scalar.copy(out=dst, in_=src)
+            else:
+                nc.vector.tensor_copy(out=dst, in_=src)
+
+        def bf(m):
+            if not live(m):
+                return
+            b, hn = m // H, m % H
+            if hn % 2 == 1:
+                if m + 1 < NH:
+                    qt_pe(m + 1)
+            elif b + 1 < B and hn > 0:
+                prep_pe(b + 1, hn // 2 - 1)
+
+        def eva(m):
+            if not live(m):
+                return
+            b, hn = m // H, m % H
+            if hn % 2 == 1:
+                if m + 1 < NH:
+                    qt_ev(m + 1, "S")
+            elif b + 1 < B and hn > 0:
+                prep_ev(b + 1, hn // 2 - 1, 0, "S")
+
+        def evb(m):
+            if not live(m):
+                return
+            b, hn = m // H, m % H
+            if hn % 2 == 0 and b + 1 < B and hn > 2:
+                prep_ev(b + 1, hn // 2 - 1, 1, "S")
+
+        def pv(m):
+            if m == 0:
+                prep_v(0)
+            if live(m) and m % H == 6 and m // H + 1 < B:
+                prep_v(m // H + 1)
+
+        def qk(n, j):
+            if not live(n):
+                return
+            t = n * NT + j
+            b, h = n // H, n % H
+            sp[t] = ps_s.tile([P, S], F32, name="sp", tag="sp")
+            nc.tensor.matmul(
+                out=sp[t][:], lhsT=qT[n // 2][:, n % 2, j, :], rhs=kT[b][:, h // (H // G), :], start=True, stop=(j >= NM)
+            )
+
+        def ta(n, j):
+            if not live(n):
+                return
+            t = n * NT + j
+            for kb in range(NT):
+                nc.tensor.matmul(
+                    out=sp[t][:, kb * P : (kb + 1) * P],
+                    lhsT=mt[n // H][:, kb, j, :],
+                    rhs=ident_f[:],
+                    start=False,
+                    stop=(kb == NT - 1),
+                    is_transpose=True,
+                )
+
+        def stt(n, j):
+            if not live(n):
+                return
+            t = n * NT + j
+            s_sb[t] = work.tile([P, S], F32, name="s_sb", tag="s_sb", bufs=4)
+            nc.vector.scalar_tensor_tensor(
+                out=s_sb[t][:].rearrange("p (t k) -> p t k", t=NT), in0=sp[t][:].rearrange("p (t k) -> p t k", t=NT), scalar=c, in1=m_sb[n // H][:, j, :].rearrange("p (k t) -> p t k", t=NT), op0=ALU.mult, op1=ALU.add
+            )
+
+        def red(n, j):
+            if not live(n):
+                return
+            t = n * NT + j
+            if j >= NM:
+                nbv[t] = work.tile([P, 1], F32, name="nbv", tag="nbv", bufs=6)
+                nc.vector.tensor_reduce(out=nbv[t][:], in_=s_sb[t][:], axis=AX.X, op=ALU.max, negate=True)
+                return
+            if n not in mx:
+                mx[n] = work.tile([P, NT], F32, name="mx", tag="mx", bufs=4)
+                nb[n] = work.tile([P, NT], F32, name="nb", tag="nb", bufs=4)
+            nc.vector.tensor_reduce(out=mx[n][:, j : j + 1], in_=sp[t][:], axis=AX.X, op=ALU.max)
+            nc.gpsimd.tensor_scalar(
+                out=nb[n][:, j : j + 1], in0=mx[n][:, j : j + 1], scalar1=-c, scalar2=0.0, op0=ALU.mult, op1=ALU.add
+            )
+
+        def ex(n, j):
+            if not live(n):
+                return
+            t = n * NT + j
+            if n not in rs:
+                rs[n] = work.tile([P, NT], F32, name="rs", tag="rs", bufs=8)
+            e_sb[t] = work.tile([P, S], BF16, name="e_sb", tag="e_sb", bufs=16)
+            if j >= NM:
+                scores, factor, bias = s_sb[t], 1.0, nbv[t][:]
+            else:
+                scores, factor, bias = sp[t], c, nb[n][:, j : j + 1]
+            nc.scalar.activation(
+                out=e_sb[t][:].rearrange("p (u k e) -> p u k e", u=2, e=2),
+                in_=scores[:].rearrange("p (u e k) -> p u k e", u=2, e=2),
+                func=ACT.Exp, bias=bias, scale=factor, accum_out=rs[n][:, j : j + 1]
+            )
+
+        def te(n, a):
+            if not live(n):
+                return
+            r = 2 * n + a
+            ep[r] = ps_e.tile([P, 2, 2, P], F32, name="ep", tag="ep")
+            for i in range(2):
+                for u in range(2):
+                    nc.tensor.transpose(
+                        out=ep[r][:, i, u, :],
+                        in_=e_sb[2 * r + i][:].bitcast(F32)[:, u * P : (u + 1) * P],
+                        identity=ident_f[:],
+                    )
+
+        def cp(n, a):
+            if not live(n):
+                return
+            r = 2 * n + a
+            grp[r] = work.tile([P, 2, P, 4], BF16, name="grp", tag="grp", bufs=8, align_bytes=64)
+            nc.scalar.copy(out=grp[r][:].bitcast(F32), in_=ep[r][:].rearrange("p a u i -> p a i u"))
+
+        def qz(n, a):
+            if not live(n):
+                return
+            r = 2 * n + a
+            codes[r] = work.tile([P, 2 * P], U32, name="codes", tag="codes", bufs=12, align_bytes=64)
+            scales[r] = work.tile([P, 2 * P], U8, name="scales", tag="scales", bufs=12, align_bytes=64)
+            nc.vector.quantize_mx(
+                out=codes[r][:].bitcast(FP8X4), scales=scales[r][:], in_=grp[r][:].rearrange("p a i t -> p (a i t)")
+            )
+
+        def mm(n):
+            if not live(n):
+                return
+            b, g = n // H, (n % H) // (H // G)
+            o_ps[n] = ps_o.tile([P, NT, D], F32, name="o_ps", tag="o_ps")
+            for j in range(NT):
+                r, a = 2 * n + j // 2, j % 2
+                nc.tensor.matmul_mx(
+                    out=o_ps[n][:, j, :],
+                    lhsT=codes[r][:, a * P : (a + 1) * P].bitcast(FP8X4),
+                    lhsT_scale=scales[r][:, a * P : (a + 1) * P],
+                    rhs=vc[b][:, g * D : (g + 1) * D].bitcast(FP8X4),
+                    rhs_scale=vs[b][:, g * D : (g + 1) * D],
+                    start=True,
+                    stop=True,
+                )
+
+        def rc(n):
+            if not live(n):
+                return
+            ri[n] = work.tile([P, NT], F32, name="ri", tag="ri", bufs=4)
+            nc.vector.reciprocal(out=ri[n][:], in_=rs[n][:])
+
+        def ov(n):
+            if not live(n):
+                return
+            o_sb = work.tile([P, NT, D], F32, name="o_sb", tag="o_sb", bufs=4)
+            nc.vector.tensor_tensor(
+                out=o_sb[:], in0=o_ps[n][:], in1=ri[n][:].unsqueeze(2).to_broadcast([P, NT, D]), op=ALU.mult
+            )
+            nc.sync.dma_start(out=out[n // H, n % H].rearrange("(p j) d -> p j d", j=NT), in_=o_sb[:])
+
+        load_k(0)
+        load_q_part(0, 2)
+        load_m(0)
+        load_q_part(2, H)
+        load_v(0)
+        load_k(1)
+        load_m(1)
+        prep_pe(0, 0)
+        qt_pe(0, ps_o, "o_ps")
+        prep_pe(0, 1, ps_e, "ep")
+        prep_pe(0, 2, ps_e, "ep")
+        prep_ev(0, 0, 0, "S")
+        qt_ev(0, "V")
+        prep_ev(0, 1, 0, "S")
+        prep_ev(0, 1, 1, "V")
+        prep_ev(0, 2, 0, "S")
+        prep_ev(0, 2, 1, "V")
+
+        for n in range(NH + 4):
+            if n < NH and n % H == 0:
+                load_q(n // H + 1)
+                load_v(n // H + 1)
+                load_k(n // H + 2)
+                load_m(n // H + 2)
+            te(n - 2, 1)
+            cp(n - 2, 0)
+            red(n - 1, 2)
+            qz(n - 3, 0)
+            red(n - 1, 3)
+            pv(n - 1)
+            ex(n - 1, 1)
+            cp(n - 2, 1)
+            bf(n)
+            ex(n - 1, 2)
+            qk(n, 0)
+            ta(n, 0)
+            qk(n, 3)
+            mm(n - 4)
+            ex(n - 1, 3)
+            red(n, 0)
+            stt(n, 3)
+            qk(n, 1)
+            ta(n, 1)
+            qz(n - 3, 1)
+            red(n, 1)
+            te(n - 1, 0)
+            eva(n)
+            qk(n, 2)
+            evb(n)
+            ta(n, 2)
+            ov(n - 4)
+            rc(n - 2)
+            ex(n, 0)

@@ -40,6 +40,9 @@ def tile_selfattention_t_kernel(tc, query_layer, key_layer, value_layer, attenti
         ident_f = const.tile([P, P], F32, name="ident_f")
         make_identity(nc, ident_f[:])
 
+        minus_one = const.tile([P, NT], F32, name="minus_one")
+        nc.gpsimd.memset(minus_one[:], -1.0)
+
         k_sb, m_sb, q_sb, v_sb = {}, {}, {}, {}
         kT, mt, vc, vs = {}, {}, {}, {}
         qT, sp, s_sb, e_sb, ep, grp, codes, scales = {}, {}, {}, {}, {}, {}, {}, {}
@@ -263,17 +266,17 @@ def tile_selfattention_t_kernel(tc, query_layer, key_layer, value_layer, attenti
             if not live(n):
                 return
             r = 2 * n + a
-            grp[r] = work.tile([P, 2, P, 4], BF16, name="grp", tag="grp", bufs=8, align_bytes=64)
-            nc.scalar.copy(out=grp[r][:].bitcast(F32), in_=ep[r][:].rearrange("p a u i -> p a i u"))
+            if a == 0:
+                grp[n] = work.tile([P, 2, 2, P, 4], BF16, name="grp", tag="grp", bufs=4, align_bytes=64)
+            nc.scalar.copy(out=grp[n][:, a, :, :, :].bitcast(F32), in_=ep[r][:].rearrange("p a u i -> p a i u"))
 
-        def qz(n, a):
+        def qz(n):
             if not live(n):
                 return
-            r = 2 * n + a
-            codes[r] = work.tile([P, 2 * P], U32, name="codes", tag="codes", bufs=12, align_bytes=64)
-            scales[r] = work.tile([P, 2 * P], U8, name="scales", tag="scales", bufs=12, align_bytes=64)
+            codes[n] = work.tile([P, NT * P], U32, name="codes", tag="codes", bufs=6, align_bytes=64)
+            scales[n] = work.tile([P, NT * P], U8, name="scales", tag="scales", bufs=6, align_bytes=64)
             nc.vector.quantize_mx(
-                out=codes[r][:].bitcast(FP8X4), scales=scales[r][:], in_=grp[r][:].rearrange("p a i t -> p (a i t)")
+                out=codes[n][:].bitcast(FP8X4), scales=scales[n][:], in_=grp[n][:].rearrange("p b a i t -> p (b a i t)")
             )
 
         def mm(n):
@@ -282,11 +285,10 @@ def tile_selfattention_t_kernel(tc, query_layer, key_layer, value_layer, attenti
             b, g = n // H, (n % H) // (H // G)
             o_ps[n] = ps_o.tile([P, NT, D], F32, name="o_ps", tag="o_ps")
             for j in range(NT):
-                r, a = 2 * n + j // 2, j % 2
                 nc.tensor.matmul_mx(
                     out=o_ps[n][:, j, :],
-                    lhsT=codes[r][:, a * P : (a + 1) * P].bitcast(FP8X4),
-                    lhsT_scale=scales[r][:, a * P : (a + 1) * P],
+                    lhsT=codes[n][:, j * P : (j + 1) * P].bitcast(FP8X4),
+                    lhsT_scale=scales[n][:, j * P : (j + 1) * P],
                     rhs=vc[b][:, g * D : (g + 1) * D].bitcast(FP8X4),
                     rhs_scale=vs[b][:, g * D : (g + 1) * D],
                     start=True,
@@ -297,7 +299,7 @@ def tile_selfattention_t_kernel(tc, query_layer, key_layer, value_layer, attenti
             if not live(n):
                 return
             ri[n] = work.tile([P, NT], F32, name="ri", tag="ri", bufs=4)
-            nc.vector.reciprocal(out=ri[n][:], in_=rs[n][:])
+            nc.gpsimd.tensor_tensor(out=ri[n][:], in0=rs[n][:], in1=minus_one[:], op=ALU.pow)
 
         def ov(n):
             if not live(n):
@@ -335,7 +337,7 @@ def tile_selfattention_t_kernel(tc, query_layer, key_layer, value_layer, attenti
             te(n - 2, 1)
             cp(n - 2, 0)
             red(n - 1, 2)
-            qz(n - 3, 0)
+            qz(n - 3)
             red(n - 1, 3)
             pv(n - 1)
             ex(n - 1, 1)
@@ -351,7 +353,6 @@ def tile_selfattention_t_kernel(tc, query_layer, key_layer, value_layer, attenti
             stt(n, 3)
             qk(n, 1)
             ta(n, 1)
-            qz(n - 3, 1)
             red(n, 1)
             te(n - 1, 0)
             eva(n)

@@ -39,6 +39,7 @@ def tile_selfattention_t_kernel(tc, query_layer, key_layer, value_layer, attenti
         make_identity(nc, ident_b[:])
         ident_f = const.tile([P, P], F32, name="ident_f")
         make_identity(nc, ident_f[:])
+        perm = const.tile([P, P], F32, name="perm")
 
         minus_one = const.tile([P, NT], F32, name="minus_one")
         nc.gpsimd.memset(minus_one[:], -1.0)
@@ -98,7 +99,7 @@ def tile_selfattention_t_kernel(tc, query_layer, key_layer, value_layer, attenti
                 for j in range(NM):
                     nc.tensor.transpose(
                         out=words[:, j * P : (j + 1) * P],
-                        in_=m_sb[b][:, j, :].bitcast(F32)[:, i - 1 : S // 2 : 2],
+                        in_=m_sb[b][:, j, :].bitcast(F32)[:, (i - 1) * P : i * P],
                         identity=ident_f[:],
                     )
 
@@ -178,8 +179,6 @@ def tile_selfattention_t_kernel(tc, query_layer, key_layer, value_layer, attenti
                 prep_ev(b + 1, hn // 2 - 1, 1, "S")
 
         def pv(m):
-            if m == 0:
-                prep_v(0)
             if live(m) and m % H == 6 and m // H + 1 < B:
                 prep_v(m // H + 1)
 
@@ -187,6 +186,8 @@ def tile_selfattention_t_kernel(tc, query_layer, key_layer, value_layer, attenti
             if not live(n):
                 return
             t = n * NT + j
+            if t in sp:
+                return
             b, h = n // H, n % H
             sp[t] = ps_s.tile([P, S], F32, name="sp", tag="sp")
             nc.tensor.matmul(
@@ -198,10 +199,11 @@ def tile_selfattention_t_kernel(tc, query_layer, key_layer, value_layer, attenti
                 return
             t = n * NT + j
             for kb in range(NT):
+                u, e = kb // 2, kb % 2
                 nc.tensor.matmul(
-                    out=sp[t][:, kb * P : (kb + 1) * P],
+                    out=sp[t][:].rearrange("p (h e k) -> p h e k", h=2, e=2)[:, :, e, u * 64 : (u + 1) * 64],
                     lhsT=mt[n // H][:, kb, j, :],
-                    rhs=ident_f[:],
+                    rhs=perm[:].rearrange("p (h r) -> p h r", h=2),
                     start=False,
                     stop=(kb == NT - 1),
                     is_transpose=True,
@@ -211,6 +213,8 @@ def tile_selfattention_t_kernel(tc, query_layer, key_layer, value_layer, attenti
             if not live(n):
                 return
             t = n * NT + j
+            if t in s_sb:
+                return
             s_sb[t] = work.tile([P, S], F32, name="s_sb", tag="s_sb", bufs=4)
             nc.vector.scalar_tensor_tensor(
                 out=s_sb[t][:].rearrange("p (t k) -> p t k", t=NT), in0=sp[t][:].rearrange("p (t k) -> p t k", t=NT), scalar=c, in1=m_sb[n // H][:, j, :].rearrange("p (k t) -> p t k", t=NT), op0=ALU.mult, op1=ALU.add
@@ -220,6 +224,8 @@ def tile_selfattention_t_kernel(tc, query_layer, key_layer, value_layer, attenti
             if not live(n):
                 return
             t = n * NT + j
+            if t in nbv:
+                return
             if j >= NM:
                 nbv[t] = work.tile([P, 1], F32, name="nbv", tag="nbv", bufs=6)
                 nc.vector.tensor_reduce(out=nbv[t][:], in_=s_sb[t][:], axis=AX.X, op=ALU.max, negate=True)
@@ -236,6 +242,8 @@ def tile_selfattention_t_kernel(tc, query_layer, key_layer, value_layer, attenti
             if not live(n):
                 return
             t = n * NT + j
+            if t in e_sb:
+                return
             if n not in rs:
                 rs[n] = work.tile([P, NT], F32, name="rs", tag="rs", bufs=8)
             e_sb[t] = work.tile([P, S], BF16, name="e_sb", tag="e_sb", bufs=16)
@@ -305,28 +313,38 @@ def tile_selfattention_t_kernel(tc, query_layer, key_layer, value_layer, attenti
             if not live(n):
                 return
             o_sb = work.tile([P, NT, D], F32, name="o_sb", tag="o_sb", bufs=4)
-            nc.vector.tensor_tensor(
-                out=o_sb[:], in0=o_ps[n][:], in1=ri[n][:].unsqueeze(2).to_broadcast([P, NT, D]), op=ALU.mult
-            )
+            if n % H == 4:
+                for j in range(NT):
+                    nc.scalar.activation(out=o_sb[:, j, :], in_=o_ps[n][:, j, :], func=ACT.Copy, scale=ri[n][:, j : j + 1])
+            else:
+                nc.vector.tensor_tensor(
+                    out=o_sb[:], in0=o_ps[n][:], in1=ri[n][:].unsqueeze(2).to_broadcast([P, NT, D]), op=ALU.mult
+                )
             nc.sync.dma_start(out=out[n // H, n % H].rearrange("(p j) d -> p j d", j=NT), in_=o_sb[:])
 
         load_k(0)
         load_q_part(0, 2)
         load_m(0)
-        load_q_part(2, H)
         load_v(0)
+        load_q_part(2, H)
         load_k(1)
         load_m(1)
         prep_pe(0, 0)
         qt_pe(0, ps_o, "o_ps")
-        prep_pe(0, 1, ps_e, "ep")
-        prep_pe(0, 2, ps_e, "ep")
         prep_ev(0, 0, 0, "S")
         qt_ev(0, "V")
+        nc.vector.tensor_copy(out=perm[:].rearrange("p (h r) -> p h r", h=2), in_=ident_f[:].rearrange("p (r h) -> p h r", h=2))
+        qk(0, 3)
+        prep_pe(0, 1, ps_e, "ep")
+        prep_pe(0, 2, ps_e, "ep")
+        stt(0, 3)
         prep_ev(0, 1, 0, "S")
         prep_ev(0, 1, 1, "V")
         prep_ev(0, 2, 0, "S")
-        prep_ev(0, 2, 1, "V")
+        prep_ev(0, 2, 1, "S")
+        red(0, 3)
+        ex(0, 3)
+        prep_v(0)
 
         for n in range(NH + 4):
             if n < NH and n % H == 0:
@@ -337,6 +355,7 @@ def tile_selfattention_t_kernel(tc, query_layer, key_layer, value_layer, attenti
             te(n - 2, 1)
             cp(n - 2, 0)
             red(n - 1, 2)
+            rc(n - 2)
             qz(n - 3)
             red(n - 1, 3)
             pv(n - 1)
@@ -360,5 +379,4 @@ def tile_selfattention_t_kernel(tc, query_layer, key_layer, value_layer, attenti
             evb(n)
             ta(n, 2)
             ov(n - 4)
-            rc(n - 2)
             ex(n, 0)

@@ -48,7 +48,7 @@ def tile_selfattention_t_kernel(tc, query_layer, key_layer, value_layer, attenti
         kT, mt, vc, vs = {}, {}, {}, {}
         qT, sp, s_sb, e_sb, ep, grp, codes, scales = {}, {}, {}, {}, {}, {}, {}, {}
         mx, nb, nbv, rs, ri, o_ps = {}, {}, {}, {}, {}, {}
-        prep = {}
+        prep, vg = {}, {}
 
         def live(n):
             return 0 <= n < NH
@@ -122,13 +122,23 @@ def tile_selfattention_t_kernel(tc, query_layer, key_layer, value_layer, attenti
             else:
                 nc.vector.tensor_scalar_mul(out=dst, in0=src, scalar1=math.sqrt(D))
 
+        def prep_vg(b, g):
+            if g == 0:
+                vg[b] = batch.tile([P, G, D, 4], BF16, name="vg", tag="vg", align_bytes=64)
+            nc.gpsimd.tensor_scalar(
+                out=vg[b][:, g, :, :],
+                in0=v_sb[b][:, g * NT : (g + 1) * NT, :].rearrange("p t d -> p d t"),
+                scalar1=1.0,
+                scalar2=0.0,
+                op0=ALU.mult,
+                op1=ALU.add,
+            )
+
         def prep_v(b):
-            vg = batch.tile([P, G, D, 4], BF16, name="vg", tag="vg", align_bytes=64)
-            nc.vector.tensor_copy(out=vg[:], in_=v_sb[b][:].rearrange("p (g t) d -> p g d t", g=G))
             vc[b] = batch.tile([P, G * D], U32, name="vc", tag="vc", align_bytes=64)
             vs[b] = batch.tile([P, G * D], U8, name="vs", tag="vs", align_bytes=64)
             nc.vector.quantize_mx(
-                out=vc[b][:].bitcast(FP8X4), scales=vs[b][:], in_=vg[:].rearrange("p g d t -> p (g d t)")
+                out=vc[b][:].bitcast(FP8X4), scales=vs[b][:], in_=vg[b][:].rearrange("p g d t -> p (g d t)")
             )
 
         def qt_pe(n, pool=None, tag="prep"):
@@ -177,6 +187,10 @@ def tile_selfattention_t_kernel(tc, query_layer, key_layer, value_layer, attenti
             b, hn = m // H, m % H
             if hn % 2 == 0 and b + 1 < B and hn > 2:
                 prep_ev(b + 1, hn // 2 - 1, 1, "S")
+
+        def pvg(m):
+            if live(m) and m % H in (4, 5) and m // H + 1 < B:
+                prep_vg(m // H + 1, m % H - 4)
 
         def pv(m):
             if live(m) and m % H == 6 and m // H + 1 < B:
@@ -313,13 +327,9 @@ def tile_selfattention_t_kernel(tc, query_layer, key_layer, value_layer, attenti
             if not live(n):
                 return
             o_sb = work.tile([P, NT, D], F32, name="o_sb", tag="o_sb", bufs=4)
-            if n % H == 4:
-                for j in range(NT):
-                    nc.scalar.activation(out=o_sb[:, j, :], in_=o_ps[n][:, j, :], func=ACT.Copy, scale=ri[n][:, j : j + 1])
-            else:
-                nc.vector.tensor_tensor(
-                    out=o_sb[:], in0=o_ps[n][:], in1=ri[n][:].unsqueeze(2).to_broadcast([P, NT, D]), op=ALU.mult
-                )
+            nc.vector.tensor_tensor(
+                out=o_sb[:], in0=o_ps[n][:], in1=ri[n][:].unsqueeze(2).to_broadcast([P, NT, D]), op=ALU.mult
+            )
             nc.sync.dma_start(out=out[n // H, n % H].rearrange("(p j) d -> p j d", j=NT), in_=o_sb[:])
 
         load_k(0)
@@ -344,6 +354,8 @@ def tile_selfattention_t_kernel(tc, query_layer, key_layer, value_layer, attenti
         prep_ev(0, 2, 1, "S")
         red(0, 3)
         ex(0, 3)
+        prep_vg(0, 0)
+        prep_vg(0, 1)
         prep_v(0)
 
         for n in range(NH + 4):
@@ -356,6 +368,7 @@ def tile_selfattention_t_kernel(tc, query_layer, key_layer, value_layer, attenti
             cp(n - 2, 0)
             red(n - 1, 2)
             rc(n - 2)
+            pvg(n - 1)
             qz(n - 3)
             red(n - 1, 3)
             pv(n - 1)

import math
from contextlib import ExitStack

import concourse.mybir as mybir
from concourse.masks import make_identity

BF16 = mybir.dt.bfloat16
F32 = mybir.dt.float32
U32 = mybir.dt.uint32
U8 = mybir.dt.uint8
FP8X4 = mybir.dt.float8_e4m3fn_x4
ALU = mybir.AluOpType
ACT = mybir.ActivationFunctionType
AX = mybir.AxisListType

B, H, G, S, D = 8, 8, 2, 512, 128
P = 128
NT = S // P
NH = B * H
NM = 3
FLOPS = 2 * 2 * B * H * S * S * D


def tile_selfattention_t_kernel(tc, query_layer, key_layer, value_layer, attention_mask, out):
    nc = tc.nc
    c = 1.0 / math.sqrt(D)
    with ExitStack() as ctx:
        ctx.enter_context(tc.manual_schedule())
        const = ctx.enter_context(tc.tile_pool(name="const", bufs=1))
        loads = ctx.enter_context(tc.tile_pool(name="loads", bufs=2))
        batch = ctx.enter_context(tc.tile_pool(name="batch", bufs=2))
        work = ctx.enter_context(tc.tile_pool(name="work", bufs=2))
        ps_s = ctx.enter_context(tc.psum_pool(name="ps_s", bufs=4))
        ps_e = ctx.enter_context(tc.psum_pool(name="ps_e", bufs=2))
        ps_o = ctx.enter_context(tc.psum_pool(name="ps_o", bufs=1))
        ps_p = ctx.enter_context(tc.psum_pool(name="ps_p", bufs=1))

        ident_b = const.tile([P, P], BF16, name="ident_b")
        make_identity(nc, ident_b[:])
        ident_f = const.tile([P, P], F32, name="ident_f")
        make_identity(nc, ident_f[:])
        perm = const.tile([P, P], F32, name="perm")

        minus_one = const.tile([P, NT], F32, name="minus_one")
        nc.gpsimd.memset(minus_one[:], -1.0)

        k_sb, m_sb, q_sb, v_sb = {}, {}, {}, {}
        kT, mt, vc, vs = {}, {}, {}, {}
        qT, sp, s_sb, e_sb, ep, grp, codes, scales = {}, {}, {}, {}, {}, {}, {}, {}
        mx, nb, nbv, rs, ri, o_ps = {}, {}, {}, {}, {}, {}
        prep, vg = {}, {}

        def live(n):
            return 0 <= n < NH

        def load_k(b):
            if b >= B:
                return
            k_sb[b] = loads.tile([P, G * NT, D], BF16, name="k_sb", tag="k_sb")
            nc.sync.dma_start(out=k_sb[b][:].rearrange("p (g t) d -> p g (t d)", t=NT), in_=key_layer[b].rearrange("g (p t) d -> p g (t d)", t=NT))

        def load_m(b):
            if b >= B:
                return
            m_sb[b] = loads.tile([P, NT, S], BF16, name="m_sb", tag="m_sb", bufs=3)
            nc.sync.dma_start(out=m_sb[b][:], in_=attention_mask[b, 0].rearrange("(p j) k -> p j k", j=NT))

        def load_q(b):
            if b >= B:
                return
            q_sb[b] = loads.tile([P, H, NT * D], BF16, name="q_sb", tag="q_sb")
            nc.sync.dma_start(out=q_sb[b][:], in_=query_layer[b].rearrange("h (p j) d -> p h (j d)", j=NT))

        def load_q_part(h0, h1):
            if h0 == 0:
                q_sb[0] = loads.tile([P, H, NT * D], BF16, name="q_sb", tag="q_sb")
            nc.sync.dma_start(
                out=q_sb[0][:, h0:h1, :], in_=query_layer[0, h0:h1].rearrange("h (p j) d -> p h (j d)", j=NT)
            )

        def load_v(b):
            if b >= B:
                return
            v_sb[b] = loads.tile([P, G * NT, D], BF16, name="v_sb", tag="v_sb")
            nc.sync.dma_start(
                out=v_sb[b][:].rearrange("p (g t) d -> p g (t d)", t=NT),
                in_=value_layer[b].rearrange("g (p t) d -> p g (t d)", t=NT),
            )

        def prep_pe(b, i, pool=None, tag="prep"):
            pt = (ps_p if pool is None else pool).tile([P, 2, NT, P], BF16, name="prep", tag=tag)
            prep[(b, i)] = pt
            if i == 0:
                for a in range(2):
                    for j in range(NT):
                        nc.tensor.transpose(out=pt[:, a, j, :], in_=k_sb[b][:, a * NT + j, :], identity=ident_b[:])
            else:
                words = pt[:].rearrange("p a j i -> p (a j i)").bitcast(F32)
                for j in range(NM):
                    nc.tensor.transpose(
                        out=words[:, j * P : (j + 1) * P],
                        in_=m_sb[b][:, j, :].bitcast(F32)[:, (i - 1) * P : i * P],
                        identity=ident_f[:],
                    )

        def prep_ev(b, i, part, eng):
            pt = prep[(b, i)]
            if i == 0:
                if part == 0:
                    kT[b] = batch.tile([P, G, S], BF16, name="kT", tag="kT")
                    dst = kT[b][:].rearrange("p g s -> p (g s)")
                    src = pt[:].rearrange("p a j i -> p (a j i)")
                    nc.scalar.copy(out=dst, in_=src)
                return
            if i == 1 and part == 0:
                mt[b] = batch.tile([P, NT, NM, P], F32, name="mt", tag="mt")
            kb = 2 * (i - 1) + part
            dst = mt[b][:, kb, :, :].rearrange("p j i -> p (j i)")
            src = pt[:].rearrange("p a j i -> p (a j i)")[:, 0 : 2 * NM * P].rearrange("p (n e) -> p n e", e=2)[:, :, part]
            if eng == "S":
                nc.scalar.mul(out=dst, in_=src, mul=math.sqrt(D))
            else:
                nc.vector.tensor_scalar_mul(out=dst, in0=src, scalar1=math.sqrt(D))

        def prep_vg(b, g):
            if g == 0:
                vg[b] = batch.tile([P, G, D, 4], BF16, name="vg", tag="vg", align_bytes=64)
            nc.gpsimd.tensor_scalar(
                out=vg[b][:, g, :, :],
                in0=v_sb[b][:, g * NT : (g + 1) * NT, :].rearrange("p t d -> p d t"),
                scalar1=1.0,
                scalar2=0.0,
                op0=ALU.mult,
                op1=ALU.add,
            )

        def prep_v(b):
            vc[b] = batch.tile([P, G * D], U32, name="vc", tag="vc", align_bytes=64)
            vs[b] = batch.tile([P, G * D], U8, name="vs", tag="vs", align_bytes=64)
            nc.vector.quantize_mx(
                out=vc[b][:].bitcast(FP8X4), scales=vs[b][:], in_=vg[b][:].rearrange("p g d t -> p (g d t)")
            )

        def qt_pe(n, pool=None, tag="prep"):
            pt = (ps_p if pool is None else pool).tile([P, 2, NT, P], BF16, name="prep", tag=tag)
            prep[("q", n)] = pt
            for a in range(2):
                for j in range(NT):
                    nc.tensor.transpose(
                        out=pt[:, a, j, :],
                        in_=q_sb[(n + a) // H][:, (n + a) % H, j * D : (j + 1) * D],
                        identity=ident_b[:],
                    )

        def qt_ev(n, eng):
            qT[n // 2] = work.tile([P, 2, NT, P], BF16, name="qT", tag="qT", bufs=3)
            dst = qT[n // 2][:].rearrange("p a j i -> p (a j i)")
            src = prep[("q", n)][:].rearrange("p a j i -> p (a j i)")
            if eng == "S":
                nc.scalar.copy(out=dst, in_=src)
            else:
                nc.vector.tensor_copy(out=dst, in_=src)

        def bf(m):
            if not live(m):
                return
            b, hn = m // H, m % H
            if hn % 2 == 1:
                if m + 1 < NH:
                    qt_pe(m + 1)
            elif b + 1 < B and hn > 0:
                prep_pe(b + 1, hn // 2 - 1)

        def eva(m):
            if not live(m):
                return
            b, hn = m // H, m % H
            if hn % 2 == 1:
                if m + 1 < NH:
                    qt_ev(m + 1, "S")
            elif b + 1 < B and hn > 0:
                prep_ev(b + 1, hn // 2 - 1, 0, "S")

        def evb(m):
            if not live(m):
                return
            b, hn = m // H, m % H
            if hn % 2 == 0 and b + 1 < B and hn > 2:
                prep_ev(b + 1, hn // 2 - 1, 1, "S")

        def pvg(m):
            if live(m) and m % H in (4, 5) and m // H + 1 < B:
                prep_vg(m // H + 1, m % H - 4)

        def pv(m):
            if live(m) and m % H == 6 and m // H + 1 < B:
                prep_v(m // H + 1)

        def qk(n, j):
            if not live(n):
                return
            t = n * NT + j
            if t in sp:
                return
            b, h = n // H, n % H
            sp[t] = ps_s.tile([P, S], F32, name="sp", tag="sp")
            nc.tensor.matmul(
                out=sp[t][:], lhsT=qT[n // 2][:, n % 2, j, :], rhs=kT[b][:, h // (H // G), :], start=True, stop=(j >= NM)
            )

        def ta(n, j):
            if not live(n):
                return
            t = n * NT + j
            for kb in range(NT):
                u, e = kb // 2, kb % 2
                nc.tensor.matmul(
                    out=sp[t][:].rearrange("p (h e k) -> p h e k", h=2, e=2)[:, :, e, u * 64 : (u + 1) * 64],
                    lhsT=mt[n // H][:, kb, j, :],
                    rhs=perm[:].rearrange("p (h r) -> p h r", h=2),
                    start=False,
                    stop=(kb == NT - 1),
                    is_transpose=True,
                )

        def stt(n, j):
            if not live(n):
                return
            t = n * NT + j
            if t in s_sb:
                return
            s_sb[t] = work.tile([P, S], F32, name="s_sb", tag="s_sb", bufs=4)
            nc.vector.scalar_tensor_tensor(
                out=s_sb[t][:].rearrange("p (t k) -> p t k", t=NT), in0=sp[t][:].rearrange("p (t k) -> p t k", t=NT), scalar=c, in1=m_sb[n // H][:, j, :].rearrange("p (k t) -> p t k", t=NT), op0=ALU.mult, op1=ALU.add
            )

        def red(n, j):
            if not live(n):
                return
            t = n * NT + j
            if t in nbv:
                return
            if j >= NM:
                nbv[t] = work.tile([P, 1], F32, name="nbv", tag="nbv", bufs=6)
                nc.vector.tensor_reduce(out=nbv[t][:], in_=s_sb[t][:], axis=AX.X, op=ALU.max, negate=True)
                return
            if n not in mx:
                mx[n] = work.tile([P, NT], F32, name="mx", tag="mx", bufs=4)
                nb[n] = work.tile([P, NT], F32, name="nb", tag="nb", bufs=4)
            nc.vector.tensor_reduce(out=mx[n][:, j : j + 1], in_=sp[t][:], axis=AX.X, op=ALU.max)
            nc.gpsimd.tensor_scalar(
                out=nb[n][:, j : j + 1], in0=mx[n][:, j : j + 1], scalar1=-c, scalar2=0.0, op0=ALU.mult, op1=ALU.add
            )

        def ex(n, j):
            if not live(n):
                return
            t = n * NT + j
            if t in e_sb:
                return
            if n not in rs:
                rs[n] = work.tile([P, NT], F32, name="rs", tag="rs", bufs=8)
            e_sb[t] = work.tile([P, S], BF16, name="e_sb", tag="e_sb", bufs=16)
            if j >= NM:
                scores, factor, bias = s_sb[t], 1.0, nbv[t][:]
            else:
                scores, factor, bias = sp[t], c, nb[n][:, j : j + 1]
            nc.scalar.activation(
                out=e_sb[t][:].rearrange("p (u k e) -> p u k e", u=2, e=2),
                in_=scores[:].rearrange("p (u e k) -> p u k e", u=2, e=2),
                func=ACT.Exp, bias=bias, scale=factor, accum_out=rs[n][:, j : j + 1]
            )

        def te(n, a):
            if not live(n):
                return
            r = 2 * n + a
            ep[r] = ps_e.tile([P, 2, 2, P], F32, name="ep", tag="ep")
            for i in range(2):
                for u in range(2):
                    nc.tensor.transpose(
                        out=ep[r][:, i, u, :],
                        in_=e_sb[2 * r + i][:].bitcast(F32)[:, u * P : (u + 1) * P],
                        identity=ident_f[:],
                    )

        def cp(n, a):
            if not live(n):
                return
            r = 2 * n + a
            if a == 0:
                grp[n] = work.tile([P, 2, 2, P, 4], BF16, name="grp", tag="grp", bufs=4, align_bytes=64)
            nc.scalar.copy(out=grp[n][:, a, :, :, :].bitcast(F32), in_=ep[r][:].rearrange("p a u i -> p a i u"))

        def qz(n):
            if not live(n):
                return
            codes[n] = work.tile([P, NT * P], U32, name="codes", tag="codes", bufs=6, align_bytes=64)
            scales[n] = work.tile([P, NT * P], U8, name="scales", tag="scales", bufs=6, align_bytes=64)
            nc.vector.quantize_mx(
                out=codes[n][:].bitcast(FP8X4), scales=scales[n][:], in_=grp[n][:].rearrange("p b a i t -> p (b a i t)")
            )

        def mm(n):
            if not live(n):
                return
            b, g = n // H, (n % H) // (H // G)
            o_ps[n] = ps_o.tile([P, NT, D], F32, name="o_ps", tag="o_ps")
            for j in range(NT):
                nc.tensor.matmul_mx(
                    out=o_ps[n][:, j, :],
                    lhsT=codes[n][:, j * P : (j + 1) * P].bitcast(FP8X4),
                    lhsT_scale=scales[n][:, j * P : (j + 1) * P],
                    rhs=vc[b][:, g * D : (g + 1) * D].bitcast(FP8X4),
                    rhs_scale=vs[b][:, g * D : (g + 1) * D],
                    start=True,
                    stop=True,
                )

        def rc(n):
            if not live(n):
                return
            ri[n] = work.tile([P, NT], F32, name="ri", tag="ri", bufs=4)
            nc.gpsimd.tensor_tensor(out=ri[n][:], in0=rs[n][:], in1=minus_one[:], op=ALU.pow)

        def ov(n):
            if not live(n):
                return
            o_sb = work.tile([P, NT, D], F32, name="o_sb", tag="o_sb", bufs=4)
            nc.vector.tensor_tensor(
                out=o_sb[:], in0=o_ps[n][:], in1=ri[n][:].unsqueeze(2).to_broadcast([P, NT, D]), op=ALU.mult
            )
            nc.sync.dma_start(out=out[n // H, n % H].rearrange("(p j) d -> p j d", j=NT), in_=o_sb[:])

        load_k(0)
        load_q_part(0, 2)
        load_m(0)
        load_v(0)
        load_q_part(2, H)
        load_k(1)
        load_m(1)
        prep_pe(0, 0)
        qt_pe(0, ps_o, "o_ps")
        prep_ev(0, 0, 0, "S")
        qt_ev(0, "V")
        nc.vector.tensor_copy(out=perm[:].rearrange("p (h r) -> p h r", h=2), in_=ident_f[:].rearrange("p (r h) -> p h r", h=2))
        qk(0, 3)
        prep_pe(0, 1, ps_e, "ep")
        prep_pe(0, 2, ps_e, "ep")
        stt(0, 3)
        prep_ev(0, 1, 0, "S")
        prep_ev(0, 1, 1, "V")
        prep_ev(0, 2, 0, "S")
        prep_ev(0, 2, 1, "S")
        red(0, 3)
        ex(0, 3)
        prep_vg(0, 0)
        prep_vg(0, 1)
        prep_v(0)

        for n in range(NH + 4):
            if n < NH and n % H == 0:
                load_q(n // H + 1)
                load_v(n // H + 1)
                load_k(n // H + 2)
                load_m(n // H + 2)
            te(n - 2, 1)
            cp(n - 2, 0)
            red(n - 1, 2)
            rc(n - 2)
            pvg(n - 1)
            qz(n - 3)
            red(n - 1, 3)
            pv(n - 1)
            ex(n - 1, 1)
            cp(n - 2, 1)
            bf(n)
            ex(n - 1, 2)
            qk(n, 0)
            ta(n, 0)
            qk(n, 3)
            mm(n - 4)
            ex(n - 1, 3)
            red(n, 0)
            stt(n, 3)
            qk(n, 1)
            ta(n, 1)
            red(n, 1)
            te(n - 1, 0)
            eva(n)
            qk(n, 2)
            evb(n)
            ta(n, 2)
            ov(n - 4)
            ex(n, 0)
